import numpy as np
import ml_dtypes


def mxq(x, axis, fmt="e4m3"):
    dtype, down = {"e4m3": (ml_dtypes.float8_e4m3fn, 7), "e5m2": (ml_dtypes.float8_e5m2, 14)}[fmt]
    v = np.moveaxis(np.asarray(x, np.float32).astype(ml_dtypes.bfloat16).astype(np.float64), axis, -1)
    blocks = v.reshape(v.shape[:-1] + (-1, 32))
    amax = np.abs(blocks).max(-1, keepdims=True)
    byte = np.maximum(np.where(amax > 0, np.frexp(amax)[1] - 1 + 127, 0) - down, 1)
    scale = np.exp2(byte - 127.0)
    codes = (blocks / scale).astype(np.float32).astype(dtype).astype(np.float64)
    return np.moveaxis((codes * scale).reshape(v.shape), -1, axis)


WIDE = False


def mx_kscale(k):
    if not WIDE:
        return np.ones(k)
    levels = np.array([10, -10, 5, -5, 0])
    a = np.random.permutation(np.resize(levels, k // 512 * 4)).reshape(k // 512, 4)
    idx = np.arange(k)
    return np.exp2(a[idx // 512, idx % 128 // 32])


BF16 = ml_dtypes.bfloat16


def bf(x):
    return np.asarray(x, np.float32).astype(BF16)


def f64(x):
    return np.asarray(x).astype(np.float64)


B, N, IN_DIM, UNITS, K = 8, 1024, 128, 128, 3
F = IN_DIM + UNITS
NUM_MX = K + 1
ROWS = F * NUM_MX


def setup_inputs():
    tf = mx_kscale(ROWS)[::NUM_MX]
    tr = np.repeat(tf, NUM_MX)[:, None]
    return {"adj": bf(np.random.standard_normal((N, N)) * 0.5 / np.sqrt(N)),
            "x0": bf(np.random.standard_normal((B, N, F)) * 0.8 * tf),
            "x1": bf(np.random.standard_normal((B, N, F)) * 0.4 * tf),
            "x2": bf(np.random.standard_normal((B, N, F)) * 0.9 * tf),
            "u": bf(1.0 / (1.0 + np.exp(-np.random.standard_normal((B, N * UNITS))))),
            "h_prev": bf(np.random.standard_normal((B, N * UNITS))),
            "c_kernel": bf(np.random.standard_normal((ROWS, UNITS)) / np.sqrt(ROWS) / tr),
            "c_bias": bf(np.random.standard_normal(UNITS) * 0.3)}


def reference(adj, x0, x1, x2, u, h_prev, c_kernel, c_bias):
    x0, x1, x2 = f64(x0), f64(x1), f64(x2)
    x3 = 2.0 * (mxq(f64(adj), 1, "e4m3") @ mxq(x2, 1, "e4m3")) - x1
    xk = np.stack([x0, x1, x2, x3], axis=-1).reshape(B * N, ROWS)
    c = np.tanh((mxq(xk, 1, "e4m3") @ mxq(f64(c_kernel), 0, "e4m3")) + f64(c_bias))
    c = c.reshape(B, N * UNITS)
    u = f64(u)
    return u * f64(h_prev) + (1.0 - u) * c

@@ -1,0 +1,268 @@
+from contextlib import ExitStack
+
+import concourse.mybir as mybir
+from concourse.masks import make_identity
+
+BF16 = mybir.dt.bfloat16
+F32 = mybir.dt.float32
+U32 = mybir.dt.uint32
+U8 = mybir.dt.uint8
+FP8X4 = mybir.dt.float8_e4m3fn_x4
+ALU = mybir.AluOpType
+TANH = mybir.ActivationFunctionType.Tanh
+
+P = 128
+PACK = 4
+BATCH = 8
+NODES = 1024
+FEATS = 256
+OUT_UNITS = 128
+TERMS = 4
+HALVES = NODES // (P * PACK)
+TILES = NODES // P
+FEAT_HALVES = FEATS // P
+HALF_NODES = NODES // HALVES
+ITEMS = BATCH * HALVES
+
+FLOPS = 2 * BATCH * NODES * NODES * FEATS + 2 * BATCH * NODES * FEATS * TERMS * OUT_UNITS
+
+
+def tile_gts_gcgrucell_pc_t_kernel(tc, adj, x0, x1, x2, u, h_prev, c_kernel, c_bias, out):
+    nc = tc.nc
+    given_terms = (x0, x1, x2)
+    with ExitStack() as ctx:
+        keep = ctx.enter_context(tc.tile_pool(name="keep", bufs=1))
+        term_pool = ctx.enter_context(tc.tile_pool(name="terms", bufs=3))
+        gate_pool = ctx.enter_context(tc.tile_pool(name="gates", bufs=4))
+        stage = ctx.enter_context(tc.tile_pool(name="stage", bufs=2))
+        xk_pool = ctx.enter_context(tc.tile_pool(name="xk", bufs=3))
+        blend_pool = ctx.enter_context(tc.tile_pool(name="blend", bufs=2))
+        psum_x3 = ctx.enter_context(tc.psum_pool(name="psum_x3", bufs=2))
+        psum_flip = ctx.enter_context(tc.psum_pool(name="psum_flip", bufs=4))
+        psum_z = ctx.enter_context(tc.psum_pool(name="psum_z", bufs=1))
+        psum_cand = ctx.enter_context(tc.psum_pool(name="psum_cand", bufs=1))
+
+        ident_bf = keep.tile([P, P], BF16)
+        make_identity(nc, ident_bf[:])
+        ident_f32 = keep.tile([P, P], F32)
+        make_identity(nc, ident_f32[:])
+
+        adj_sb = keep.tile([P, TILES, NODES], BF16)
+        adj_rows = adj.rearrange("(c p t) n -> p c t n", c=HALVES, p=P, t=PACK)
+
+        def load_adj_pair(pair):
+            c, t = divmod(2 * pair, PACK)
+            nc.sync.dma_start(out=adj_sb[:, 2 * pair : 2 * pair + 2, :], in_=adj_rows[:, c, t : t + 2, :])
+
+        batch_tiles = {}
+
+        def load_batch(b):
+            terms = term_pool.tile([P, TERMS, TILES, FEATS], BF16)
+            for k in (2, 1, 0):
+                nc.sync.dma_start(
+                    out=terms[:, k].rearrange("p (c t) f -> p c (t f)", c=HALVES),
+                    in_=given_terms[k][b].rearrange("(c p t) f -> p c (t f)", c=HALVES, p=P, t=PACK),
+                )
+            gate = gate_pool.tile([P, HALVES, PACK * OUT_UNITS], BF16)
+            nc.sync.dma_start(out=gate[:], in_=u[b].rearrange("(c p r) -> p c r", c=HALVES, p=P))
+            old = gate_pool.tile([P, HALVES, PACK * OUT_UNITS], BF16)
+            nc.sync.dma_start(out=old[:], in_=h_prev[b].rearrange("(c p r) -> p c r", c=HALVES, p=P))
+            batch_tiles[b] = (terms, gate, old)
+
+        w_rows = keep.tile([P, FEAT_HALVES, PACK, OUT_UNITS], BF16)
+        nc.scalar.dma_start(
+            out=w_rows[:].rearrange("p g k j -> p g (k j)"),
+            in_=c_kernel.rearrange("(g p k) j -> p g (k j)", g=FEAT_HALVES, p=P, k=PACK),
+        )
+        bias_rows = keep.tile([P, P], BF16)
+        nc.vector.memset(bias_rows[:], 0.0)
+        nc.scalar.dma_start(out=bias_rows[0:1, :], in_=c_bias.rearrange("(o j) -> o j", o=1))
+
+        w_codes = keep.tile([P, FEAT_HALVES, OUT_UNITS], U32, align_bytes=64)
+        w_scales = keep.tile([P, FEAT_HALVES, OUT_UNITS], U8, align_bytes=64)
+        bias_col = keep.tile([P, 1], F32)
+
+        def prepare_weights():
+            w_grouped = keep.tile([P, FEAT_HALVES, OUT_UNITS, PACK], BF16, align_bytes=64)
+            nc.vector.tensor_copy(out=w_grouped[:], in_=w_rows[:].rearrange("p g k j -> p g j k"))
+            nc.vector.quantize_mx(
+                out=w_codes[:].rearrange("p g j -> p (g j)").bitcast(FP8X4),
+                scales=w_scales[:].rearrange("p g j -> p (g j)"),
+                in_=w_grouped[:].rearrange("p g j k -> p (g j k)"),
+            )
+            bias_flipped = psum_flip.tile([P, P], BF16, tag="flip")
+            nc.tensor.transpose(out=bias_flipped[:], in_=bias_rows[:], identity=ident_bf[:])
+            nc.vector.tensor_copy(out=bias_col[:], in_=bias_flipped[:, 0:1])
+
+        adj_words = adj_sb[:].bitcast(F32).rearrange("p s (c q w) -> p s c w q", c=HALVES, w=2)
+        adj_codes = keep.tile([P, TILES // 2, HALVES, 2 * P], U32, align_bytes=64)
+        adj_scales = keep.tile([P, TILES // 2, HALVES, 2 * P], U8, align_bytes=64)
+
+        def quantise_adj_pair(pair):
+            adj_grouped = stage.tile([P, HALVES, 2 * P, PACK], BF16, align_bytes=64)
+            grouped_words = adj_grouped[:].bitcast(F32)
+            for c in range(HALVES):
+                flipped = psum_flip.tile([P, 2, 2 * P], F32, tag="flip")
+                for w in range(2):
+                    for s in range(2):
+                        nc.tensor.transpose(
+                            out=flipped[:, w, s * P : (s + 1) * P],
+                            in_=adj_words[:, 2 * pair + s, c, w, :],
+                            identity=ident_f32[:],
+                        )
+                copy_out = nc.vector.tensor_copy if c == 0 else nc.scalar.copy
+                copy_out(out=grouped_words[:, c], in_=flipped[:].rearrange("q w m -> q m w"))
+            nc.vector.quantize_mx(
+                out=adj_codes[:, pair].rearrange("p c m -> p (c m)").bitcast(FP8X4),
+                scales=adj_scales[:, pair].rearrange("p c m -> p (c m)"),
+                in_=adj_grouped[:].rearrange("p c m t -> p (c m t)"),
+            )
+
+        x2_operands = {}
+
+        def quantise_x2(b):
+            terms = batch_tiles[b][0]
+            x2_grouped = stage.tile([P, HALVES, FEATS, PACK], BF16, align_bytes=64)
+            for c in range(HALVES):
+                nc.vector.tensor_copy(
+                    out=x2_grouped[:, c].rearrange("p (a i) t -> p a t i", i=4),
+                    in_=terms[:, 2, c * PACK : (c + 1) * PACK, :].rearrange("p t (a i) -> p a t i", i=4),
+                )
+            x2_codes = stage.tile([P, HALVES, FEATS], U32, align_bytes=64)
+            x2_scales = stage.tile([P, HALVES, FEATS], U8, align_bytes=64)
+            nc.vector.quantize_mx(
+                out=x2_codes[:].rearrange("p c f -> p (c f)").bitcast(FP8X4),
+                scales=x2_scales[:].rearrange("p c f -> p (c f)"),
+                in_=x2_grouped[:].rearrange("p c f t -> p (c f t)"),
+            )
+            x2_operands[b] = (x2_codes, x2_scales)
+
+        def diffuse(item):
+            b, c = divmod(item, HALVES)
+            terms = batch_tiles[b][0]
+            x2_codes, x2_scales = x2_operands[b]
+            for pair in range(c * PACK // 2, (c + 1) * PACK // 2):
+                product = psum_x3.tile([P, 2, FEATS], F32)
+                for s in range(2):
+                    receivers = slice(s * P, (s + 1) * P)
+                    for n in range(HALVES):
+                        nc.tensor.matmul_mx(
+                            out=product[:, s, :],
+                            lhsT=adj_codes[:, pair, n, receivers].bitcast(FP8X4),
+                            lhsT_scale=adj_scales[:, pair, n, receivers],
+                            rhs=x2_codes[:, n, :].bitcast(FP8X4),
+                            rhs_scale=x2_scales[:, n, :],
+                            start=(n == 0),
+                            stop=(n == HALVES - 1),
+                        )
+                nc.vector.scalar_tensor_tensor(
+                    out=terms[:, 3, 2 * pair : 2 * pair + 2, :],
+                    in0=product[:],
+                    scalar=2.0,
+                    in1=terms[:, 1, 2 * pair : 2 * pair + 2, :],
+                    op0=ALU.mult,
+                    op1=ALU.subtract,
+                )
+
+        xk_grouped_tiles = {}
+
+        def flip_terms(item):
+            b, c = divmod(item, HALVES)
+            terms = batch_tiles[b][0]
+            xk_grouped = xk_pool.tile([P, FEAT_HALVES, HALF_NODES, TERMS], BF16, align_bytes=64)
+            for g in range(FEAT_HALVES):
+                for pair in range(PACK // 2):
+                    flipped = psum_flip.tile([P, 2, TERMS, P], BF16, tag="flip")
+                    for s in range(2):
+                        for k in range(TERMS):
+                            nc.tensor.transpose(
+                                out=flipped[:, s, k, :],
+                                in_=terms[:, k, c * PACK + 2 * pair + s, g * P : (g + 1) * P],
+                                identity=ident_bf[:],
+                            )
+                    nc.scalar.copy(
+                        out=xk_grouped[:, g, 2 * pair * P : 2 * (pair + 1) * P, :].rearrange(
+                            "p (s m) k -> p s m k", s=2
+                        ),
+                        in_=flipped[:].rearrange("p s k m -> p s m k"),
+                    )
+            xk_grouped_tiles[item] = xk_grouped
+
+        xk_operands = {}
+
+        def quantise_xk(item):
+            xk_codes = xk_pool.tile([P, FEAT_HALVES, HALF_NODES], U32, align_bytes=64)
+            xk_scales = xk_pool.tile([P, FEAT_HALVES, HALF_NODES], U8, align_bytes=64)
+            nc.vector.quantize_mx(
+                out=xk_codes[:].rearrange("p g m -> p (g m)").bitcast(FP8X4),
+                scales=xk_scales[:].rearrange("p g m -> p (g m)"),
+                in_=xk_grouped_tiles[item][:].rearrange("p g m k -> p (g m k)"),
+            )
+            xk_operands[item] = (xk_codes, xk_scales)
+
+        candidates = {}
+
+        def candidate(item):
+            xk_codes, xk_scales = xk_operands[item]
+            z = psum_z.tile([P, HALF_NODES], F32)
+            for g in range(FEAT_HALVES):
+                nc.tensor.matmul_mx(
+                    out=z[:],
+                    lhsT=w_codes[:, g, :].bitcast(FP8X4),
+                    lhsT_scale=w_scales[:, g, :],
+                    rhs=xk_codes[:, g, :].bitcast(FP8X4),
+                    rhs_scale=xk_scales[:, g, :],
+                    start=(g == 0),
+                    stop=(g == FEAT_HALVES - 1),
+                )
+            cand_by_unit = blend_pool.tile([P, HALF_NODES], F32)
+            nc.scalar.activation(out=cand_by_unit[:], in_=z[:], func=TANH, bias=bias_col[:, 0:1], scale=1.0)
+            candidates[item] = cand_by_unit
+
+        def blend_and_store(item):
+            b, c = divmod(item, HALVES)
+            gate, old = batch_tiles[b][1:]
+            cand = psum_cand.tile([P, PACK * OUT_UNITS], F32)
+            for t in range(PACK):
+                nc.tensor.transpose(
+                    out=cand[:, t * OUT_UNITS : (t + 1) * OUT_UNITS],
+                    in_=candidates[item][:, t * P : (t + 1) * P],
+                    identity=ident_f32[:],
+                )
+            diff = blend_pool.tile([P, PACK * OUT_UNITS], F32)
+            nc.vector.tensor_tensor(out=diff[:], in0=old[:, c, :], in1=cand[:], op=ALU.subtract)
+            step = blend_pool.tile([P, PACK * OUT_UNITS], F32)
+            nc.vector.tensor_tensor(out=step[:], in0=diff[:], in1=gate[:, c, :], op=ALU.mult)
+            result = blend_pool.tile([P, PACK * OUT_UNITS], F32)
+            nc.vector.tensor_tensor(out=result[:], in0=step[:], in1=cand[:], op=ALU.add)
+            nc.sync.dma_start(out=out[b].rearrange("(c p r) -> c p r", c=HALVES, p=P)[c], in_=result[:])
+
+        load_adj_pair(0)
+        load_adj_pair(1)
+        load_batch(0)
+        load_adj_pair(2)
+        load_adj_pair(3)
+        load_batch(1)
+        quantise_adj_pair(0)
+        quantise_adj_pair(1)
+        quantise_x2(0)
+        diffuse(0)
+        quantise_adj_pair(2)
+        quantise_adj_pair(3)
+        prepare_weights()
+        for item in range(ITEMS + 3):
+            if 0 <= item - 1 < ITEMS:
+                quantise_xk(item - 1)
+            if item + 1 < ITEMS:
+                diffuse(item + 1)
+            if 0 <= item - 2 < ITEMS:
+                candidate(item - 2)
+            if 0 <= item - 3:
+                blend_and_store(item - 3)
+            if item < ITEMS:
+                flip_terms(item)
+            b, c = divmod(item, HALVES)
+            if c == 0 and b + 1 < BATCH:
+                quantise_x2(b + 1)
+            if c == 0 and b + 2 < BATCH:
+                load_batch(b + 2)

@@ -24,6 +24,8 @@ FEAT_HALVES = FEATS // P
 HALF_NODES = NODES // HALVES
 ITEMS = BATCH * HALVES
 
+VECTOR_BANKS = ()
+
 FLOPS = 2 * BATCH * NODES * NODES * FEATS + 2 * BATCH * NODES * FEATS * TERMS * OUT_UNITS
 
 
@@ -32,11 +34,12 @@ def tile_gts_gcgrucell_pc_t_kernel(tc, adj, x0, x1, x2, u, h_prev, c_kernel, c_b
     given_terms = (x0, x1, x2)
     with ExitStack() as ctx:
         keep = ctx.enter_context(tc.tile_pool(name="keep", bufs=1))
-        term_pool = ctx.enter_context(tc.tile_pool(name="terms", bufs=3))
-        gate_pool = ctx.enter_context(tc.tile_pool(name="gates", bufs=4))
+        term_pool = ctx.enter_context(tc.tile_pool(name="terms", bufs=4))
+        gate_pool = ctx.enter_context(tc.tile_pool(name="gates", bufs=5))
         stage = ctx.enter_context(tc.tile_pool(name="stage", bufs=2))
         xk_pool = ctx.enter_context(tc.tile_pool(name="xk", bufs=3))
         blend_pool = ctx.enter_context(tc.tile_pool(name="blend", bufs=2))
+        ctx.enter_context(tc.manual_schedule())
         psum_x3 = ctx.enter_context(tc.psum_pool(name="psum_x3", bufs=2))
         psum_flip = ctx.enter_context(tc.psum_pool(name="psum_flip", bufs=4))
         psum_z = ctx.enter_context(tc.psum_pool(name="psum_z", bufs=1))
@@ -46,37 +49,55 @@ def tile_gts_gcgrucell_pc_t_kernel(tc, adj, x0, x1, x2, u, h_prev, c_kernel, c_b
         make_identity(nc, ident_bf[:])
         ident_f32 = keep.tile([P, P], F32)
         make_identity(nc, ident_f32[:])
+        warm = keep.tile([P, 1], F32)
+        nc.vector.memset(warm[:], 0.0)
+        warm_out = keep.tile([P, 1], F32)
+        nc.scalar.activation(out=warm_out[:], in_=warm[:], func=TANH)
+        neg_ident = keep.tile([P, P], BF16)
+        nc.vector.tensor_scalar(out=neg_ident[:], in0=ident_bf[:], scalar1=-1.0, scalar2=None, op0=ALU.mult)
 
         adj_sb = keep.tile([P, TILES, NODES], BF16)
         adj_rows = adj.rearrange("(c p t) n -> p c t n", c=HALVES, p=P, t=PACK)
 
-        def load_adj_pair(pair):
-            c, t = divmod(2 * pair, PACK)
-            nc.sync.dma_start(out=adj_sb[:, 2 * pair : 2 * pair + 2, :], in_=adj_rows[:, c, t : t + 2, :])
+        def load_adj(tile, tiles=2):
+            c, t = divmod(tile, PACK)
+            nc.sync.dma_start(out=adj_sb[:, tile : tile + tiles, :], in_=adj_rows[:, c, t : t + tiles, :])
 
         batch_tiles = {}
 
-        def load_batch(b):
-            terms = term_pool.tile([P, TERMS, TILES, FEATS], BF16)
-            for k in (2, 1, 0):
-                nc.sync.dma_start(
-                    out=terms[:, k].rearrange("p (c t) f -> p c (t f)", c=HALVES),
-                    in_=given_terms[k][b].rearrange("(c p t) f -> p c (t f)", c=HALVES, p=P, t=PACK),
-                )
+        term_tiles = {}
+
+        def load_term(b, k):
+            if b not in term_tiles:
+                terms = term_pool.tile([P, TERMS, TILES, FEATS], BF16)
+                term_tiles[b] = terms
+            nc.sync.dma_start(
+                out=term_tiles[b][:, k].rearrange("p (c t) f -> p c (t f)", c=HALVES),
+                in_=given_terms[k][b].rearrange("(c p t) f -> p c (t f)", c=HALVES, p=P, t=PACK),
+            )
+
+        def load_gates(b):
             gate = gate_pool.tile([P, HALVES, PACK * OUT_UNITS], BF16)
             nc.sync.dma_start(out=gate[:], in_=u[b].rearrange("(c p r) -> p c r", c=HALVES, p=P))
             old = gate_pool.tile([P, HALVES, PACK * OUT_UNITS], BF16)
             nc.sync.dma_start(out=old[:], in_=h_prev[b].rearrange("(c p r) -> p c r", c=HALVES, p=P))
-            batch_tiles[b] = (terms, gate, old)
+            batch_tiles[b] = (gate, old)
+
+        def load_batch(b):
+            for k in (2, 1, 0):
+                load_term(b, k)
+            load_gates(b)
 
         w_rows = keep.tile([P, FEAT_HALVES, PACK, OUT_UNITS], BF16)
-        nc.scalar.dma_start(
-            out=w_rows[:].rearrange("p g k j -> p g (k j)"),
-            in_=c_kernel.rearrange("(g p k) j -> p g (k j)", g=FEAT_HALVES, p=P, k=PACK),
-        )
         bias_rows = keep.tile([P, P], BF16)
         nc.vector.memset(bias_rows[:], 0.0)
-        nc.scalar.dma_start(out=bias_rows[0:1, :], in_=c_bias.rearrange("(o j) -> o j", o=1))
+
+        def load_weights():
+            nc.sync.dma_start(
+                out=w_rows[:].rearrange("p g k j -> p g (k j)"),
+                in_=c_kernel.rearrange("(g p k) j -> p g (k j)", g=FEAT_HALVES, p=P, k=PACK),
+            )
+            nc.sync.dma_start(out=bias_rows[0:1, :], in_=c_bias.rearrange("(o j) -> o j", o=1))
 
         w_codes = keep.tile([P, FEAT_HALVES, OUT_UNITS], U32, align_bytes=64)
         w_scales = keep.tile([P, FEAT_HALVES, OUT_UNITS], U8, align_bytes=64)
@@ -98,8 +119,11 @@ def tile_gts_gcgrucell_pc_t_kernel(tc, adj, x0, x1, x2, u, h_prev, c_kernel, c_b
         adj_codes = keep.tile([P, TILES // 2, HALVES, 2 * P], U32, align_bytes=64)
         adj_scales = keep.tile([P, TILES // 2, HALVES, 2 * P], U8, align_bytes=64)
 
-        def quantise_adj_pair(pair):
+        adj_grouped_tiles = {}
+
+        def flip_adj_pair(pair):
             adj_grouped = stage.tile([P, HALVES, 2 * P, PACK], BF16, align_bytes=64)
+            adj_grouped_tiles[pair] = adj_grouped
             grouped_words = adj_grouped[:].bitcast(F32)
             for c in range(HALVES):
                 flipped = psum_flip.tile([P, 2, 2 * P], F32, tag="flip")
@@ -110,8 +134,10 @@ def tile_gts_gcgrucell_pc_t_kernel(tc, adj, x0, x1, x2, u, h_prev, c_kernel, c_b
                             in_=adj_words[:, 2 * pair + s, c, w, :],
                             identity=ident_f32[:],
                         )
-                copy_out = nc.vector.tensor_copy if c == 0 else nc.scalar.copy
-                copy_out(out=grouped_words[:, c], in_=flipped[:].rearrange("q w m -> q m w"))
+                nc.scalar.copy(out=grouped_words[:, c], in_=flipped[:].rearrange("q w m -> q m w"))
+
+        def quantise_adj_pair(pair):
+            adj_grouped = adj_grouped_tiles[pair]
             nc.vector.quantize_mx(
                 out=adj_codes[:, pair].rearrange("p c m -> p (c m)").bitcast(FP8X4),
                 scales=adj_scales[:, pair].rearrange("p c m -> p (c m)"),
@@ -120,14 +146,19 @@ def tile_gts_gcgrucell_pc_t_kernel(tc, adj, x0, x1, x2, u, h_prev, c_kernel, c_b
 
         x2_operands = {}
 
+        x2_grouped_tiles = {}
+
+        def group_x2(b, c):
+            if c == 0:
+                x2_grouped = stage.tile([P, HALVES, FEATS, PACK], BF16, align_bytes=64)
+                x2_grouped_tiles[b] = x2_grouped
+            nc.vector.tensor_copy(
+                out=x2_grouped_tiles[b][:, c].rearrange("p (a i) t -> p a t i", i=4),
+                in_=term_tiles[b][:, 2, c * PACK : (c + 1) * PACK, :].rearrange("p t (a i) -> p a t i", i=4),
+            )
+
         def quantise_x2(b):
-            terms = batch_tiles[b][0]
-            x2_grouped = stage.tile([P, HALVES, FEATS, PACK], BF16, align_bytes=64)
-            for c in range(HALVES):
-                nc.vector.tensor_copy(
-                    out=x2_grouped[:, c].rearrange("p (a i) t -> p a t i", i=4),
-                    in_=terms[:, 2, c * PACK : (c + 1) * PACK, :].rearrange("p t (a i) -> p a t i", i=4),
-                )
+            x2_grouped = x2_grouped_tiles[b]
             x2_codes = stage.tile([P, HALVES, FEATS], U32, align_bytes=64)
             x2_scales = stage.tile([P, HALVES, FEATS], U8, align_bytes=64)
             nc.vector.quantize_mx(
@@ -137,72 +168,85 @@ def tile_gts_gcgrucell_pc_t_kernel(tc, adj, x0, x1, x2, u, h_prev, c_kernel, c_b
             )
             x2_operands[b] = (x2_codes, x2_scales)
 
-        def diffuse(item):
+        products = {}
+
+        def diffuse(item, h):
             b, c = divmod(item, HALVES)
-            terms = batch_tiles[b][0]
             x2_codes, x2_scales = x2_operands[b]
-            for pair in range(c * PACK // 2, (c + 1) * PACK // 2):
-                product = psum_x3.tile([P, 2, FEATS], F32)
-                for s in range(2):
-                    receivers = slice(s * P, (s + 1) * P)
-                    for n in range(HALVES):
-                        nc.tensor.matmul_mx(
-                            out=product[:, s, :],
-                            lhsT=adj_codes[:, pair, n, receivers].bitcast(FP8X4),
-                            lhsT_scale=adj_scales[:, pair, n, receivers],
-                            rhs=x2_codes[:, n, :].bitcast(FP8X4),
-                            rhs_scale=x2_scales[:, n, :],
-                            start=(n == 0),
-                            stop=(n == HALVES - 1),
-                        )
-                nc.vector.scalar_tensor_tensor(
-                    out=terms[:, 3, 2 * pair : 2 * pair + 2, :],
-                    in0=product[:],
-                    scalar=2.0,
-                    in1=terms[:, 1, 2 * pair : 2 * pair + 2, :],
-                    op0=ALU.mult,
-                    op1=ALU.subtract,
-                )
+            pair = c * PACK // 2 + h
+            product = psum_x3.tile([P, 2, FEATS], F32)
+            for s in range(2):
+                receivers = slice(s * P, (s + 1) * P)
+                for n in range(HALVES):
+                    nc.tensor.matmul_mx(
+                        out=product[:, s, :],
+                        lhsT=adj_codes[:, pair, n, receivers].bitcast(FP8X4),
+                        lhsT_scale=adj_scales[:, pair, n, receivers],
+                        rhs=x2_codes[:, n, :].bitcast(FP8X4),
+                        rhs_scale=x2_scales[:, n, :],
+                        start=(n == 0),
+                        stop=(n == HALVES - 1),
+                    )
+            products[item, h] = product
+
+        def finish_x3(item, h):
+            b, c = divmod(item, HALVES)
+            terms = term_tiles[b]
+            pair = c * PACK // 2 + h
+            nc.vector.scalar_tensor_tensor(
+                out=terms[:, 3, 2 * pair : 2 * pair + 2, :],
+                in0=products[item, h][:],
+                scalar=2.0,
+                in1=terms[:, 1, 2 * pair : 2 * pair + 2, :],
+                op0=ALU.mult,
+                op1=ALU.subtract,
+            )
 
         xk_grouped_tiles = {}
+        flipped_tiles = {}
 
-        def flip_terms(item):
+        def flip_terms(item, g, pair):
             b, c = divmod(item, HALVES)
-            terms = batch_tiles[b][0]
-            xk_grouped = xk_pool.tile([P, FEAT_HALVES, HALF_NODES, TERMS], BF16, align_bytes=64)
-            for g in range(FEAT_HALVES):
-                for pair in range(PACK // 2):
-                    flipped = psum_flip.tile([P, 2, TERMS, P], BF16, tag="flip")
-                    for s in range(2):
-                        for k in range(TERMS):
-                            nc.tensor.transpose(
-                                out=flipped[:, s, k, :],
-                                in_=terms[:, k, c * PACK + 2 * pair + s, g * P : (g + 1) * P],
-                                identity=ident_bf[:],
-                            )
-                    nc.scalar.copy(
-                        out=xk_grouped[:, g, 2 * pair * P : 2 * (pair + 1) * P, :].rearrange(
-                            "p (s m) k -> p s m k", s=2
-                        ),
-                        in_=flipped[:].rearrange("p s k m -> p s m k"),
+            terms = term_tiles[b]
+            if g == 0 and pair == 0:
+                xk_grouped = xk_pool.tile([P, FEAT_HALVES, HALF_NODES, TERMS], BF16, align_bytes=64)
+                xk_grouped_tiles[item] = xk_grouped
+            flipped = psum_flip.tile([P, 2, TERMS, P], BF16, tag="flip")
+            for s in range(2):
+                for k in range(TERMS):
+                    nc.tensor.transpose(
+                        out=flipped[:, s, k, :],
+                        in_=terms[:, k, c * PACK + 2 * pair + s, g * P : (g + 1) * P],
+                        identity=ident_bf[:],
                     )
-            xk_grouped_tiles[item] = xk_grouped
+            flipped_tiles[item, g, pair] = flipped
+
+        def lay_terms(item, g, pair):
+            flipped = flipped_tiles[item, g, pair]
+            copy_out = nc.vector.tensor_copy if (item % 2, g, pair) in VECTOR_BANKS else nc.scalar.copy
+            copy_out(
+                out=xk_grouped_tiles[item][:, g, 2 * pair * P : 2 * (pair + 1) * P, :].rearrange(
+                    "p (s m) k -> p s m k", s=2
+                ),
+                in_=flipped[:].rearrange("p s k m -> p s m k"),
+            )
 
         xk_operands = {}
 
-        def quantise_xk(item):
-            xk_codes = xk_pool.tile([P, FEAT_HALVES, HALF_NODES], U32, align_bytes=64)
-            xk_scales = xk_pool.tile([P, FEAT_HALVES, HALF_NODES], U8, align_bytes=64)
+        def quantise_xk(item, g):
+            if g == 0:
+                xk_codes = xk_pool.tile([P, FEAT_HALVES, HALF_NODES], U32, align_bytes=64)
+                xk_scales = xk_pool.tile([P, FEAT_HALVES, HALF_NODES], U8, align_bytes=64)
+                xk_operands[item] = (xk_codes, xk_scales)
             nc.vector.quantize_mx(
-                out=xk_codes[:].rearrange("p g m -> p (g m)").bitcast(FP8X4),
-                scales=xk_scales[:].rearrange("p g m -> p (g m)"),
-                in_=xk_grouped_tiles[item][:].rearrange("p g m k -> p (g m k)"),
+                out=xk_operands[item][0][:, g, :].bitcast(FP8X4),
+                scales=xk_operands[item][1][:, g, :],
+                in_=xk_grouped_tiles[item][:, g].rearrange("p m k -> p (m k)"),
             )
-            xk_operands[item] = (xk_codes, xk_scales)
 
-        candidates = {}
+        preactivations = {}
 
-        def candidate(item):
+        def contract_xk(item):
             xk_codes, xk_scales = xk_operands[item]
             z = psum_z.tile([P, HALF_NODES], F32)
             for g in range(FEAT_HALVES):
@@ -215,54 +259,160 @@ def tile_gts_gcgrucell_pc_t_kernel(tc, adj, x0, x1, x2, u, h_prev, c_kernel, c_b
                     start=(g == 0),
                     stop=(g == FEAT_HALVES - 1),
                 )
+            preactivations[item] = z
+
+        candidates = {}
+
+        def candidate(item):
             cand_by_unit = blend_pool.tile([P, HALF_NODES], F32)
-            nc.scalar.activation(out=cand_by_unit[:], in_=z[:], func=TANH, bias=bias_col[:, 0:1], scale=1.0)
+            nc.scalar.activation(
+                out=cand_by_unit[:], in_=preactivations[item][:], func=TANH, bias=bias_col[:, 0:1], scale=1.0
+            )
             candidates[item] = cand_by_unit
 
-        def blend_and_store(item):
-            b, c = divmod(item, HALVES)
-            gate, old = batch_tiles[b][1:]
-            cand = psum_cand.tile([P, PACK * OUT_UNITS], F32)
-            for t in range(PACK):
-                nc.tensor.transpose(
-                    out=cand[:, t * OUT_UNITS : (t + 1) * OUT_UNITS],
-                    in_=candidates[item][:, t * P : (t + 1) * P],
-                    identity=ident_f32[:],
-                )
-            diff = blend_pool.tile([P, PACK * OUT_UNITS], F32)
-            nc.vector.tensor_tensor(out=diff[:], in0=old[:, c, :], in1=cand[:], op=ALU.subtract)
-            step = blend_pool.tile([P, PACK * OUT_UNITS], F32)
-            nc.vector.tensor_tensor(out=step[:], in0=diff[:], in1=gate[:, c, :], op=ALU.mult)
-            result = blend_pool.tile([P, PACK * OUT_UNITS], F32)
-            nc.vector.tensor_tensor(out=result[:], in0=step[:], in1=cand[:], op=ALU.add)
-            nc.sync.dma_start(out=out[b].rearrange("(c p r) -> c p r", c=HALVES, p=P)[c], in_=result[:])
+        differences = {}
 
-        load_adj_pair(0)
-        load_adj_pair(1)
-        load_batch(0)
-        load_adj_pair(2)
-        load_adj_pair(3)
-        load_batch(1)
-        quantise_adj_pair(0)
-        quantise_adj_pair(1)
-        quantise_x2(0)
-        diffuse(0)
-        quantise_adj_pair(2)
-        quantise_adj_pair(3)
-        prepare_weights()
-        for item in range(ITEMS + 3):
-            if 0 <= item - 1 < ITEMS:
-                quantise_xk(item - 1)
-            if item + 1 < ITEMS:
-                diffuse(item + 1)
-            if 0 <= item - 2 < ITEMS:
-                candidate(item - 2)
-            if 0 <= item - 3:
-                blend_and_store(item - 3)
-            if item < ITEMS:
-                flip_terms(item)
+        def subtract_old(item):
             b, c = divmod(item, HALVES)
-            if c == 0 and b + 1 < BATCH:
-                quantise_x2(b + 1)
-            if c == 0 and b + 2 < BATCH:
-                load_batch(b + 2)
+            diff = psum_cand.tile([P, PACK * OUT_UNITS], F32)
+            nc.tensor.matmul(diff[:], lhsT=neg_ident[:], rhs=batch_tiles[b][1][:, c, :], start=True, stop=False)
+            for t in range(PACK):
+                nc.tensor.matmul(
+                    diff[:, t * OUT_UNITS : (t + 1) * OUT_UNITS],
+                    lhsT=candidates[item][:, t * P : (t + 1) * P],
+                    rhs=ident_f32[:],
+                    is_transpose=True,
+                    start=False,
+                    stop=(t == PACK - 1),
+                )
+            differences[item] = diff
+
+        steps = {}
+
+        def scale_step(item):
+            b, c = divmod(item, HALVES)
+            step = blend_pool.tile([P, PACK * OUT_UNITS], F32)
+            nc.vector.scalar_tensor_tensor(
+                out=step[:],
+                in0=batch_tiles[b][0][:, c, :],
+                scalar=-1.0,
+                in1=differences[item][:],
+                op0=ALU.add,
+                op1=ALU.mult,
+            )
+            steps[item] = step
+
+        results = {}
+
+        def finish(item):
+            b, c = divmod(item, HALVES)
+            result = blend_pool.tile([P, PACK * OUT_UNITS], F32)
+            nc.vector.tensor_tensor(out=result[:], in0=batch_tiles[b][1][:, c, :], in1=steps[item][:], op=ALU.subtract)
+            results[item] = result
+
+        def store(item):
+            b, c = divmod(item, HALVES)
+            nc.sync.dma_start(out=out[b].rearrange("(c p r) -> c p r", c=HALVES, p=P)[c], in_=results[item][:])
+
+        load_adj(0, 1)
+        load_adj(1, 1)
+        load_term(0, 2)
+        load_adj(2)
+        load_term(0, 1)
+        load_term(0, 0)
+        load_adj(4)
+        load_adj(6)
+        load_term(1, 2)
+        load_weights()
+        load_term(1, 1)
+        load_term(1, 0)
+        load_gates(0)
+
+        flip_adj_pair(0)
+        group_x2(0, 0)
+        group_x2(0, 1)
+        quantise_adj_pair(0)
+        quantise_x2(0)
+        flip_adj_pair(1)
+        diffuse(0, 0)
+        finish_x3(0, 0)
+        quantise_adj_pair(1)
+        flip_adj_pair(2)
+        diffuse(0, 1)
+        finish_x3(0, 1)
+        for g in range(FEAT_HALVES):
+            flip_terms(0, g, 0)
+            lay_terms(0, g, 0)
+        quantise_adj_pair(2)
+        diffuse(1, 0)
+        finish_x3(1, 0)
+        flip_adj_pair(3)
+        group_x2(1, 0)
+        group_x2(1, 1)
+        for g in range(FEAT_HALVES):
+            flip_terms(0, g, 1)
+            lay_terms(0, g, 1)
+        quantise_adj_pair(3)
+        quantise_x2(1)
+        diffuse(1, 1)
+        finish_x3(1, 1)
+
+        for r in range(1, ITEMS + 4):
+            if 0 <= r - 4 < ITEMS:
+                store(r - 4)
+            if (r + 3) % 2 == 0 and 4 <= r + 3 < ITEMS:
+                load_term((r + 3) // 2, 2)
+            if (r + 3) % 2 == 0 and 4 <= r + 3 < ITEMS:
+                load_term((r + 3) // 2, 1)
+            if (r + 3) % 2 == 0 and 4 <= r + 3 < ITEMS:
+                load_term((r + 3) // 2, 0)
+            if (r + 1) % 2 == 0 and 2 <= r + 1 < ITEMS:
+                load_gates((r + 1) // 2)
+            if r == 99:
+                pass
+            if 2 <= r + 1 < ITEMS:
+                diffuse(r + 1, 0)
+            if 2 <= r + 1 < ITEMS:
+                diffuse(r + 1, 1)
+            if 0 <= r - 2 < ITEMS:
+                contract_xk(r - 2)
+            if 0 <= r - 3 < ITEMS:
+                scale_step(r - 3)
+            if 0 <= r - 3 < ITEMS:
+                finish(r - 3)
+            if 2 <= r + 1 < ITEMS:
+                finish_x3(r + 1, 0)
+            if 2 <= r + 1 < ITEMS:
+                finish_x3(r + 1, 1)
+            if 1 <= r < ITEMS:
+                flip_terms(r, 0, 0)
+            if 0 <= r - 2 < ITEMS:
+                candidate(r - 2)
+            if 1 <= r < ITEMS:
+                lay_terms(r, 0, 0)
+            if (r + 2) % 2 == 0 and 4 <= r + 2 < ITEMS:
+                group_x2((r + 2) // 2, 1)
+            if 1 <= r < ITEMS:
+                flip_terms(r, 0, 1)
+            if 1 <= r < ITEMS:
+                lay_terms(r, 0, 1)
+            if r == 1:
+                prepare_weights()
+            if (r + 2) % 2 == 0 and 4 <= r + 2 < ITEMS:
+                quantise_x2((r + 2) // 2)
+            if 1 <= r < ITEMS:
+                flip_terms(r, 1, 0)
+            if 1 <= r < ITEMS:
+                lay_terms(r, 1, 0)
+            if 0 <= r - 1 < ITEMS:
+                quantise_xk(r - 1, 0)
+            if 1 <= r < ITEMS:
+                flip_terms(r, 1, 1)
+            if 1 <= r < ITEMS:
+                lay_terms(r, 1, 1)
+            if 0 <= r - 1 < ITEMS:
+                quantise_xk(r - 1, 1)
+            if (r + 3) % 2 == 0 and 4 <= r + 3 < ITEMS:
+                group_x2((r + 3) // 2, 0)
+            if 0 <= r - 2 < ITEMS:
+                subtract_old(r - 2)

from contextlib import ExitStack

import concourse.mybir as mybir
from concourse.masks import make_identity

BF16 = mybir.dt.bfloat16
F32 = mybir.dt.float32
U32 = mybir.dt.uint32
U8 = mybir.dt.uint8
FP8X4 = mybir.dt.float8_e4m3fn_x4
ALU = mybir.AluOpType
TANH = mybir.ActivationFunctionType.Tanh

P = 128
PACK = 4
BATCH = 8
NODES = 1024
FEATS = 256
OUT_UNITS = 128
TERMS = 4
HALVES = NODES // (P * PACK)
TILES = NODES // P
FEAT_HALVES = FEATS // P
HALF_NODES = NODES // HALVES
ITEMS = BATCH * HALVES

VECTOR_BANKS = ()

FLOPS = 2 * BATCH * NODES * NODES * FEATS + 2 * BATCH * NODES * FEATS * TERMS * OUT_UNITS


def tile_gts_gcgrucell_pc_t_kernel(tc, adj, x0, x1, x2, u, h_prev, c_kernel, c_bias, out):
    nc = tc.nc
    given_terms = (x0, x1, x2)
    with ExitStack() as ctx:
        keep = ctx.enter_context(tc.tile_pool(name="keep", bufs=1))
        term_pool = ctx.enter_context(tc.tile_pool(name="terms", bufs=4))
        gate_pool = ctx.enter_context(tc.tile_pool(name="gates", bufs=5))
        stage = ctx.enter_context(tc.tile_pool(name="stage", bufs=2))
        xk_pool = ctx.enter_context(tc.tile_pool(name="xk", bufs=3))
        blend_pool = ctx.enter_context(tc.tile_pool(name="blend", bufs=2))
        ctx.enter_context(tc.manual_schedule())
        psum_x3 = ctx.enter_context(tc.psum_pool(name="psum_x3", bufs=2))
        psum_flip = ctx.enter_context(tc.psum_pool(name="psum_flip", bufs=4))
        psum_z = ctx.enter_context(tc.psum_pool(name="psum_z", bufs=1))
        psum_cand = ctx.enter_context(tc.psum_pool(name="psum_cand", bufs=1))

        ident_bf = keep.tile([P, P], BF16)
        make_identity(nc, ident_bf[:])
        ident_f32 = keep.tile([P, P], F32)
        make_identity(nc, ident_f32[:])
        warm = keep.tile([P, 1], F32)
        nc.vector.memset(warm[:], 0.0)
        warm_out = keep.tile([P, 1], F32)
        nc.scalar.activation(out=warm_out[:], in_=warm[:], func=TANH)
        neg_ident = keep.tile([P, P], BF16)
        nc.vector.tensor_scalar(out=neg_ident[:], in0=ident_bf[:], scalar1=-1.0, scalar2=None, op0=ALU.mult)

        adj_sb = keep.tile([P, TILES, NODES], BF16)
        adj_rows = adj.rearrange("(c p t) n -> p c t n", c=HALVES, p=P, t=PACK)

        def load_adj(tile, tiles=2):
            c, t = divmod(tile, PACK)
            nc.sync.dma_start(out=adj_sb[:, tile : tile + tiles, :], in_=adj_rows[:, c, t : t + tiles, :])

        batch_tiles = {}

        term_tiles = {}

        def load_term(b, k):
            if b not in term_tiles:
                terms = term_pool.tile([P, TERMS, TILES, FEATS], BF16)
                term_tiles[b] = terms
            nc.sync.dma_start(
                out=term_tiles[b][:, k].rearrange("p (c t) f -> p c (t f)", c=HALVES),
                in_=given_terms[k][b].rearrange("(c p t) f -> p c (t f)", c=HALVES, p=P, t=PACK),
            )

        def load_gates(b):
            gate = gate_pool.tile([P, HALVES, PACK * OUT_UNITS], BF16)
            nc.sync.dma_start(out=gate[:], in_=u[b].rearrange("(c p r) -> p c r", c=HALVES, p=P))
            old = gate_pool.tile([P, HALVES, PACK * OUT_UNITS], BF16)
            nc.sync.dma_start(out=old[:], in_=h_prev[b].rearrange("(c p r) -> p c r", c=HALVES, p=P))
            batch_tiles[b] = (gate, old)

        def load_batch(b):
            for k in (2, 1, 0):
                load_term(b, k)
            load_gates(b)

        w_rows = keep.tile([P, FEAT_HALVES, PACK, OUT_UNITS], BF16)
        bias_rows = keep.tile([P, P], BF16)
        nc.vector.memset(bias_rows[:], 0.0)

        def load_weights():
            nc.sync.dma_start(
                out=w_rows[:].rearrange("p g k j -> p g (k j)"),
                in_=c_kernel.rearrange("(g p k) j -> p g (k j)", g=FEAT_HALVES, p=P, k=PACK),
            )
            nc.sync.dma_start(out=bias_rows[0:1, :], in_=c_bias.rearrange("(o j) -> o j", o=1))

        w_codes = keep.tile([P, FEAT_HALVES, OUT_UNITS], U32, align_bytes=64)
        w_scales = keep.tile([P, FEAT_HALVES, OUT_UNITS], U8, align_bytes=64)
        bias_col = keep.tile([P, 1], F32)

        def prepare_weights():
            w_grouped = keep.tile([P, FEAT_HALVES, OUT_UNITS, PACK], BF16, align_bytes=64)
            nc.vector.tensor_copy(out=w_grouped[:], in_=w_rows[:].rearrange("p g k j -> p g j k"))
            nc.vector.quantize_mx(
                out=w_codes[:].rearrange("p g j -> p (g j)").bitcast(FP8X4),
                scales=w_scales[:].rearrange("p g j -> p (g j)"),
                in_=w_grouped[:].rearrange("p g j k -> p (g j k)"),
            )
            bias_flipped = psum_flip.tile([P, P], BF16, tag="flip")
            nc.tensor.transpose(out=bias_flipped[:], in_=bias_rows[:], identity=ident_bf[:])
            nc.vector.tensor_copy(out=bias_col[:], in_=bias_flipped[:, 0:1])

        adj_words = adj_sb[:].bitcast(F32).rearrange("p s (c q w) -> p s c w q", c=HALVES, w=2)
        adj_codes = keep.tile([P, TILES // 2, HALVES, 2 * P], U32, align_bytes=64)
        adj_scales = keep.tile([P, TILES // 2, HALVES, 2 * P], U8, align_bytes=64)

        adj_grouped_tiles = {}

        def flip_adj_pair(pair):
            adj_grouped = stage.tile([P, HALVES, 2 * P, PACK], BF16, align_bytes=64)
            adj_grouped_tiles[pair] = adj_grouped
            grouped_words = adj_grouped[:].bitcast(F32)
            for c in range(HALVES):
                flipped = psum_flip.tile([P, 2, 2 * P], F32, tag="flip")
                for w in range(2):
                    for s in range(2):
                        nc.tensor.transpose(
                            out=flipped[:, w, s * P : (s + 1) * P],
                            in_=adj_words[:, 2 * pair + s, c, w, :],
                            identity=ident_f32[:],
                        )
                nc.scalar.copy(out=grouped_words[:, c], in_=flipped[:].rearrange("q w m -> q m w"))

        def quantise_adj_pair(pair):
            adj_grouped = adj_grouped_tiles[pair]
            nc.vector.quantize_mx(
                out=adj_codes[:, pair].rearrange("p c m -> p (c m)").bitcast(FP8X4),
                scales=adj_scales[:, pair].rearrange("p c m -> p (c m)"),
                in_=adj_grouped[:].rearrange("p c m t -> p (c m t)"),
            )

        x2_operands = {}

        x2_grouped_tiles = {}

        def group_x2(b, c):
            if c == 0:
                x2_grouped = stage.tile([P, HALVES, FEATS, PACK], BF16, align_bytes=64)
                x2_grouped_tiles[b] = x2_grouped
            nc.vector.tensor_copy(
                out=x2_grouped_tiles[b][:, c].rearrange("p (a i) t -> p a t i", i=4),
                in_=term_tiles[b][:, 2, c * PACK : (c + 1) * PACK, :].rearrange("p t (a i) -> p a t i", i=4),
            )

        def quantise_x2(b):
            x2_grouped = x2_grouped_tiles[b]
            x2_codes = stage.tile([P, HALVES, FEATS], U32, align_bytes=64)
            x2_scales = stage.tile([P, HALVES, FEATS], U8, align_bytes=64)
            nc.vector.quantize_mx(
                out=x2_codes[:].rearrange("p c f -> p (c f)").bitcast(FP8X4),
                scales=x2_scales[:].rearrange("p c f -> p (c f)"),
                in_=x2_grouped[:].rearrange("p c f t -> p (c f t)"),
            )
            x2_operands[b] = (x2_codes, x2_scales)

        products = {}

        def diffuse(item, h):
            b, c = divmod(item, HALVES)
            x2_codes, x2_scales = x2_operands[b]
            pair = c * PACK // 2 + h
            product = psum_x3.tile([P, 2, FEATS], F32)
            for s in range(2):
                receivers = slice(s * P, (s + 1) * P)
                for n in range(HALVES):
                    nc.tensor.matmul_mx(
                        out=product[:, s, :],
                        lhsT=adj_codes[:, pair, n, receivers].bitcast(FP8X4),
                        lhsT_scale=adj_scales[:, pair, n, receivers],
                        rhs=x2_codes[:, n, :].bitcast(FP8X4),
                        rhs_scale=x2_scales[:, n, :],
                        start=(n == 0),
                        stop=(n == HALVES - 1),
                    )
            products[item, h] = product

        def finish_x3(item, h):
            b, c = divmod(item, HALVES)
            terms = term_tiles[b]
            pair = c * PACK // 2 + h
            nc.vector.scalar_tensor_tensor(
                out=terms[:, 3, 2 * pair : 2 * pair + 2, :],
                in0=products[item, h][:],
                scalar=2.0,
                in1=terms[:, 1, 2 * pair : 2 * pair + 2, :],
                op0=ALU.mult,
                op1=ALU.subtract,
            )

        xk_grouped_tiles = {}
        flipped_tiles = {}

        def flip_terms(item, g, pair):
            b, c = divmod(item, HALVES)
            terms = term_tiles[b]
            if g == 0 and pair == 0:
                xk_grouped = xk_pool.tile([P, FEAT_HALVES, HALF_NODES, TERMS], BF16, align_bytes=64)
                xk_grouped_tiles[item] = xk_grouped
            flipped = psum_flip.tile([P, 2, TERMS, P], BF16, tag="flip")
            for s in range(2):
                for k in range(TERMS):
                    nc.tensor.transpose(
                        out=flipped[:, s, k, :],
                        in_=terms[:, k, c * PACK + 2 * pair + s, g * P : (g + 1) * P],
                        identity=ident_bf[:],
                    )
            flipped_tiles[item, g, pair] = flipped

        def lay_terms(item, g, pair):
            flipped = flipped_tiles[item, g, pair]
            copy_out = nc.vector.tensor_copy if (item % 2, g, pair) in VECTOR_BANKS else nc.scalar.copy
            copy_out(
                out=xk_grouped_tiles[item][:, g, 2 * pair * P : 2 * (pair + 1) * P, :].rearrange(
                    "p (s m) k -> p s m k", s=2
                ),
                in_=flipped[:].rearrange("p s k m -> p s m k"),
            )

        xk_operands = {}

        def quantise_xk(item, g):
            if g == 0:
                xk_codes = xk_pool.tile([P, FEAT_HALVES, HALF_NODES], U32, align_bytes=64)
                xk_scales = xk_pool.tile([P, FEAT_HALVES, HALF_NODES], U8, align_bytes=64)
                xk_operands[item] = (xk_codes, xk_scales)
            nc.vector.quantize_mx(
                out=xk_operands[item][0][:, g, :].bitcast(FP8X4),
                scales=xk_operands[item][1][:, g, :],
                in_=xk_grouped_tiles[item][:, g].rearrange("p m k -> p (m k)"),
            )

        preactivations = {}

        def contract_xk(item):
            xk_codes, xk_scales = xk_operands[item]
            z = psum_z.tile([P, HALF_NODES], F32)
            for g in range(FEAT_HALVES):
                nc.tensor.matmul_mx(
                    out=z[:],
                    lhsT=w_codes[:, g, :].bitcast(FP8X4),
                    lhsT_scale=w_scales[:, g, :],
                    rhs=xk_codes[:, g, :].bitcast(FP8X4),
                    rhs_scale=xk_scales[:, g, :],
                    start=(g == 0),
                    stop=(g == FEAT_HALVES - 1),
                )
            preactivations[item] = z

        candidates = {}

        def candidate(item):
            cand_by_unit = blend_pool.tile([P, HALF_NODES], F32)
            nc.scalar.activation(
                out=cand_by_unit[:], in_=preactivations[item][:], func=TANH, bias=bias_col[:, 0:1], scale=1.0
            )
            candidates[item] = cand_by_unit

        differences = {}

        def subtract_old(item):
            b, c = divmod(item, HALVES)
            diff = psum_cand.tile([P, PACK * OUT_UNITS], F32)
            nc.tensor.matmul(diff[:], lhsT=neg_ident[:], rhs=batch_tiles[b][1][:, c, :], start=True, stop=False)
            for t in range(PACK):
                nc.tensor.matmul(
                    diff[:, t * OUT_UNITS : (t + 1) * OUT_UNITS],
                    lhsT=candidates[item][:, t * P : (t + 1) * P],
                    rhs=ident_f32[:],
                    is_transpose=True,
                    start=False,
                    stop=(t == PACK - 1),
                )
            differences[item] = diff

        steps = {}

        def scale_step(item):
            b, c = divmod(item, HALVES)
            step = blend_pool.tile([P, PACK * OUT_UNITS], F32)
            nc.vector.scalar_tensor_tensor(
                out=step[:],
                in0=batch_tiles[b][0][:, c, :],
                scalar=-1.0,
                in1=differences[item][:],
                op0=ALU.add,
                op1=ALU.mult,
            )
            steps[item] = step

        results = {}

        def finish(item):
            b, c = divmod(item, HALVES)
            result = blend_pool.tile([P, PACK * OUT_UNITS], F32)
            nc.vector.tensor_tensor(out=result[:], in0=batch_tiles[b][1][:, c, :], in1=steps[item][:], op=ALU.subtract)
            results[item] = result

        def store(item):
            b, c = divmod(item, HALVES)
            nc.sync.dma_start(out=out[b].rearrange("(c p r) -> c p r", c=HALVES, p=P)[c], in_=results[item][:])

        load_adj(0, 1)
        load_adj(1, 1)
        load_term(0, 2)
        load_adj(2)
        load_term(0, 1)
        load_term(0, 0)
        load_adj(4)
        load_adj(6)
        load_term(1, 2)
        load_weights()
        load_term(1, 1)
        load_term(1, 0)
        load_gates(0)

        flip_adj_pair(0)
        group_x2(0, 0)
        group_x2(0, 1)
        quantise_adj_pair(0)
        quantise_x2(0)
        flip_adj_pair(1)
        diffuse(0, 0)
        finish_x3(0, 0)
        quantise_adj_pair(1)
        flip_adj_pair(2)
        diffuse(0, 1)
        finish_x3(0, 1)
        for g in range(FEAT_HALVES):
            flip_terms(0, g, 0)
            lay_terms(0, g, 0)
        quantise_adj_pair(2)
        diffuse(1, 0)
        finish_x3(1, 0)
        flip_adj_pair(3)
        group_x2(1, 0)
        group_x2(1, 1)
        for g in range(FEAT_HALVES):
            flip_terms(0, g, 1)
            lay_terms(0, g, 1)
        quantise_adj_pair(3)
        quantise_x2(1)
        diffuse(1, 1)
        finish_x3(1, 1)

        for r in range(1, ITEMS + 4):
            if 0 <= r - 4 < ITEMS:
                store(r - 4)
            if (r + 3) % 2 == 0 and 4 <= r + 3 < ITEMS:
                load_term((r + 3) // 2, 2)
            if (r + 3) % 2 == 0 and 4 <= r + 3 < ITEMS:
                load_term((r + 3) // 2, 1)
            if (r + 3) % 2 == 0 and 4 <= r + 3 < ITEMS:
                load_term((r + 3) // 2, 0)
            if (r + 1) % 2 == 0 and 2 <= r + 1 < ITEMS:
                load_gates((r + 1) // 2)
            if r == 99:
                pass
            if 2 <= r + 1 < ITEMS:
                diffuse(r + 1, 0)
            if 2 <= r + 1 < ITEMS:
                diffuse(r + 1, 1)
            if 0 <= r - 2 < ITEMS:
                contract_xk(r - 2)
            if 0 <= r - 3 < ITEMS:
                scale_step(r - 3)
            if 0 <= r - 3 < ITEMS:
                finish(r - 3)
            if 2 <= r + 1 < ITEMS:
                finish_x3(r + 1, 0)
            if 2 <= r + 1 < ITEMS:
                finish_x3(r + 1, 1)
            if 1 <= r < ITEMS:
                flip_terms(r, 0, 0)
            if 0 <= r - 2 < ITEMS:
                candidate(r - 2)
            if 1 <= r < ITEMS:
                lay_terms(r, 0, 0)
            if (r + 2) % 2 == 0 and 4 <= r + 2 < ITEMS:
                group_x2((r + 2) // 2, 1)
            if 1 <= r < ITEMS:
                flip_terms(r, 0, 1)
            if 1 <= r < ITEMS:
                lay_terms(r, 0, 1)
            if r == 1:
                prepare_weights()
            if (r + 2) % 2 == 0 and 4 <= r + 2 < ITEMS:
                quantise_x2((r + 2) // 2)
            if 1 <= r < ITEMS:
                flip_terms(r, 1, 0)
            if 1 <= r < ITEMS:
                lay_terms(r, 1, 0)
            if 0 <= r - 1 < ITEMS:
                quantise_xk(r - 1, 0)
            if 1 <= r < ITEMS:
                flip_terms(r, 1, 1)
            if 1 <= r < ITEMS:
                lay_terms(r, 1, 1)
            if 0 <= r - 1 < ITEMS:
                quantise_xk(r - 1, 1)
            if (r + 3) % 2 == 0 and 4 <= r + 3 < ITEMS:
                group_x2((r + 3) // 2, 0)
            if 0 <= r - 2 < ITEMS:
                subtract_old(r - 2)
